import numpy as np
import ml_dtypes


def mxq(x, axis, fmt="e4m3"):
    dtype, down = {"e4m3": (ml_dtypes.float8_e4m3fn, 7), "e5m2": (ml_dtypes.float8_e5m2, 14)}[fmt]
    v = np.moveaxis(np.asarray(x, np.float32).astype(ml_dtypes.bfloat16).astype(np.float64), axis, -1)
    blocks = v.reshape(v.shape[:-1] + (-1, 32))
    amax = np.abs(blocks).max(-1, keepdims=True)
    byte = np.maximum(np.where(amax > 0, np.frexp(amax)[1] - 1 + 127, 0) - down, 1)
    scale = np.exp2(byte - 127.0)
    codes = (blocks / scale).astype(np.float32).astype(dtype).astype(np.float64)
    return np.moveaxis((codes * scale).reshape(v.shape), -1, axis)


WIDE = False


def mx_kscale(k):
    if not WIDE:
        return np.ones(k)
    levels = np.array([10, -10, 5, -5, 0])
    if k % 512:
        return np.exp2(np.random.permutation(np.resize(levels, k // 32))).repeat(32)
    a = np.empty((k // 512, 16))
    for p in range(k // 512):
        a[p, :8] = np.random.permutation(np.resize(levels, 8))
        for g in range(8):
            far = levels[np.abs(levels - a[p, g]) >= 10]
            a[p, g + 8] = far[np.random.randint(len(far))]
    return np.exp2(a.ravel()).repeat(32)


BF16 = ml_dtypes.bfloat16


def bf(x):
    return np.asarray(x, np.float32).astype(BF16)


def f64(x):
    return np.asarray(x).astype(np.float64)


BATCH, OUTPUT_R, KERNEL, INPUT_DEPTH, OUTPUT_DEPTH, SIX = 1024, 2, 8, 8, 64, 6
INPUT_R = OUTPUT_R * KERNEL
P = OUTPUT_R ** 2
G = OUTPUT_DEPTH * SIX
W = KERNEL ** 2 * INPUT_DEPTH
ROWS = P * G
COLS = INPUT_R ** 2 * INPUT_DEPTH
IDX = np.arange(COLS).reshape(OUTPUT_R, KERNEL, OUTPUT_R, KERNEL * INPUT_DEPTH).transpose(0, 2, 1, 3).reshape(P, W)


def setup_inputs():
    s = mx_kscale(W)
    sc = np.empty(COLS)
    sc[IDX] = s
    c = np.mean(1.0 / s)
    window = np.zeros((P, COLS))
    window[np.arange(P)[:, None], IDX] = 1.0
    return {"x": bf(np.random.standard_normal((BATCH, COLS)) * 0.2 * np.sqrt(W) * c * sc),
            "connect_w": bf(np.random.standard_normal((ROWS, COLS))),
            "connect_mask": bf(np.random.uniform(0.5, 1.5, (ROWS, COLS)) * np.repeat(window, G, axis=0) / sc)}


def reference(x, connect_w, connect_mask):
    w = np.exp(f64(connect_w)) * f64(connect_mask)
    w = w / np.sum(w, axis=-1, keepdims=True)
    xw = f64(x)[:, IDX].transpose(1, 0, 2)
    ww = np.take_along_axis(w.reshape(P, G, COLS), IDX[:, None, :], axis=2)
    out = mxq(xw, 2, "e4m3") @ mxq(ww, 2, "e4m3").transpose(0, 2, 1)
    return out.transpose(1, 0, 2).reshape(BATCH, -1, SIX)

@@ -1,0 +1,215 @@
+from contextlib import ExitStack
+
+import concourse.mybir as mybir
+from concourse.masks import make_identity
+
+F32 = mybir.dt.float32
+BF16 = mybir.dt.bfloat16
+U32 = mybir.dt.uint32
+U8 = mybir.dt.uint8
+FP8X4 = mybir.dt.float8_e4m3fn_x4
+ACT = mybir.ActivationFunctionType
+ALU = mybir.AluOpType
+
+P = 128
+PACK = 4
+K = P * PACK
+BANK = 512
+
+BATCH = 1024
+COLS = 2048
+PIXEL_ROWS = 16
+ROW = COLS // PIXEL_ROWS
+RUN = ROW // 2
+WINDOW_ROWS = PIXEL_ROWS // 2
+WINDOWS = 4
+G = 384
+OUT_COLS = WINDOWS * G
+HALF = COLS // 2
+SPAN = HALF - RUN
+
+W_TILES = OUT_COLS // P
+X_TILES = BATCH // P
+BANKS_OUT = OUT_COLS // BANK
+
+CUTS = sorted(set(range(0, OUT_COLS + 1, G)) | set(range(0, OUT_COLS + 1, BANK // 2)))
+
+FLOPS = 2 * BATCH * OUT_COLS * K
+BYTES = 2 * BATCH * COLS + 2 * 2 * OUT_COLS * K + 4 * BATCH * OUT_COLS
+
+
+def window_view(half_rows):
+    return half_rows[:].rearrange("g (a s) -> g a s", s=ROW)[:, :, 0:RUN]
+
+
+def tile_connectlayer_kernel(tc, x, connect_w, connect_mask, out):
+    nc = tc.nc
+    out_rows = out.rearrange("b r s -> b (r s)")
+
+    with ExitStack() as ctx:
+        const = ctx.enter_context(tc.tile_pool(name="const", bufs=1))
+        loads = ctx.enter_context(tc.tile_pool(name="loads", bufs=1))
+        keep = ctx.enter_context(tc.tile_pool(name="keep", bufs=1))
+        work = ctx.enter_context(tc.tile_pool(name="work", bufs=3))
+        results = ctx.enter_context(tc.tile_pool(name="results", bufs=4))
+        transposed = ctx.enter_context(tc.psum_pool(name="transposed", bufs=3))
+        sums = ctx.enter_context(tc.psum_pool(name="sums", bufs=5))
+        ctx.enter_context(tc.manual_schedule())
+
+        cw_in = []
+        mask_in = []
+        for r in range(W_TILES):
+            i, j = divmod(r * P // G, 2)
+            rows = slice(r * P, (r + 1) * P)
+            cols = slice(i * HALF + j * RUN, i * HALF + j * RUN + SPAN)
+            cw_t = loads.tile([P, HALF], BF16, name="cw%d" % r)
+            nc.sync.dma_start(out=cw_t[:, 0:SPAN], in_=connect_w[rows, cols])
+            mask_t = loads.tile([P, HALF], BF16, name="mask%d" % r)
+            nc.sync.dma_start(out=mask_t[:, 0:SPAN], in_=connect_mask[rows, cols])
+            cw_in.append(cw_t)
+            mask_in.append(mask_t)
+        x_in = []
+        for n in range(X_TILES):
+            x_t = loads.tile([P, COLS], BF16, name="x%d" % n)
+            nc.sync.dma_start(out=x_t[:], in_=x[n * P : (n + 1) * P, :])
+            x_in.append(x_t)
+
+        ident_f32 = const.tile([P, P], F32, name="ident_f32")
+        make_identity(nc, ident_f32[:])
+
+        w_codes = keep.tile([P, OUT_COLS], U32, name="w_codes", align_bytes=64)
+        w_scales = keep.tile([P, OUT_COLS], U8, name="w_scales", align_bytes=64)
+
+        expw, prod, rowsum, rinv, w_bf, wt, w_grouped = {}, {}, {}, {}, {}, {}, {}
+        xc, xt, x_grouped, x_codes, x_scales, acc, result = {}, {}, {}, {}, {}, {}, {}
+
+        def exponential(r):
+            expw[r] = work.tile([P, WINDOW_ROWS, RUN], F32, name="expw")
+            nc.scalar.activation(out=expw[r][:], in_=window_view(cw_in[r]), func=ACT.Exp)
+
+        def product_and_rowsum(r):
+            prod[r] = work.tile([P, WINDOW_ROWS, RUN], F32, name="prod")
+            rowsum[r] = work.tile([P, 1], F32, name="rowsum")
+            nc.vector.scalar_tensor_tensor(
+                out=prod[r][:],
+                in0=expw[r][:],
+                scalar=1.0,
+                in1=window_view(mask_in[r]),
+                op0=ALU.mult,
+                op1=ALU.mult,
+                accum_out=rowsum[r][:],
+            )
+
+        def reciprocal(r):
+            rinv[r] = work.tile([P, 1], F32, name="rinv")
+            nc.vector.reciprocal(out=rinv[r][:], in_=rowsum[r][:])
+
+        def normalise(r):
+            w_bf[r] = work.tile([P, K], BF16, name="w_bf")
+            nc.vector.tensor_scalar(
+                out=w_bf[r][:].rearrange("g (u q e) -> g u q e", u=2, e=2),
+                in0=prod[r][:].rearrange("g a c -> g (a c)").rearrange("g (q u e) -> g u q e", u=2, e=2),
+                scalar1=rinv[r][:, 0:1],
+                scalar2=None,
+                op0=ALU.mult,
+            )
+
+        def transpose_w(r):
+            wt[r] = transposed.tile([P, 2, P], F32, name="wt", tag="bank")
+            words = w_bf[r][:].bitcast(F32)
+            for u in range(2):
+                nc.tensor.transpose(wt[r][:, u, :], words[:, u * P : (u + 1) * P], ident_f32[:])
+
+        def regroup_w(r):
+            w_grouped[r] = work.tile([P, K], BF16, name="w_grouped", align_bytes=64)
+            nc.scalar.copy(
+                out=w_grouped[r][:].bitcast(F32).rearrange("q (g u) -> q g u", u=2),
+                in_=wt[r][:].rearrange("q u g -> q g u"),
+            )
+
+        def quantise_w(r):
+            nc.vector.quantize_mx(
+                out=w_codes[:, r * P : (r + 1) * P].bitcast(FP8X4),
+                scales=w_scales[:, r * P : (r + 1) * P],
+                in_=w_grouped[r][:],
+            )
+
+        def gather_windows(n):
+            xc[n] = work.tile([P, COLS], BF16, name="xc")
+            for j in range(2):
+                nc.vector.tensor_copy(
+                    out=xc[n][:].bitcast(F32)[:, j * BANK : (j + 1) * BANK].rearrange(
+                        "b (u r s) -> b u r s", u=2, r=PIXEL_ROWS
+                    ),
+                    in_=x_in[n][:].bitcast(F32).rearrange("b (r j s u) -> b j u r s", r=PIXEL_ROWS, j=2, u=2)[:, j],
+                )
+
+        def transpose_x(n):
+            xc_words = xc[n][:].bitcast(F32)
+            for j in range(2):
+                xt[n, j] = transposed.tile([P, PACK, P], F32, name="xt", tag="bank")
+                for i in range(2):
+                    for u in range(2):
+                        first = ((j * 2 + u) * 2 + i) * P
+                        nc.tensor.transpose(xt[n, j][:, i * 2 + u, :], xc_words[:, first : first + P], ident_f32[:])
+
+        def regroup_x(n):
+            x_grouped[n] = work.tile([P, COLS], BF16, name="x_grouped", align_bytes=64)
+            xg_words = x_grouped[n][:].bitcast(F32)
+            for j in range(2):
+                nc.scalar.copy(
+                    out=xg_words[:, j * BANK : (j + 1) * BANK].rearrange("q (i b u) -> q i b u", i=2, u=2),
+                    in_=xt[n, j][:].rearrange("q (i u) b -> q i b u", u=2),
+                )
+
+        def quantise_x(n):
+            x_codes[n] = work.tile([P, BANK], U32, name="x_codes", align_bytes=64)
+            x_scales[n] = work.tile([P, BANK], U8, name="x_scales", align_bytes=64)
+            nc.vector.quantize_mx(out=x_codes[n][:].bitcast(FP8X4), scales=x_scales[n][:], in_=x_grouped[n][:])
+
+        def multiply(n):
+            acc[n] = [sums.tile([P, BANK], F32, name="acc%d" % b, tag="acc") for b in range(BANKS_OUT)]
+            for c0, c1 in zip(CUTS[:-1], CUTS[1:]):
+                i, j = divmod(c0 // G, 2)
+                slot = slice((2 * j + i) * P, (2 * j + i + 1) * P)
+                b = c0 // BANK
+                nc.tensor.matmul_mx(
+                    out=acc[n][b][:, c0 - b * BANK : c1 - b * BANK],
+                    lhsT=x_codes[n][:, slot].bitcast(FP8X4),
+                    lhsT_scale=x_scales[n][:, slot],
+                    rhs=w_codes[:, c0:c1].bitcast(FP8X4),
+                    rhs_scale=w_scales[:, c0:c1],
+                    start=True,
+                    stop=True,
+                )
+
+        def empty_and_store(n):
+            result[n] = results.tile([P, OUT_COLS], F32, name="result")
+            for b in range(BANKS_OUT):
+                cols = slice(b * BANK, (b + 1) * BANK)
+                if (n * BANKS_OUT + b) % 2 == 0:
+                    nc.scalar.copy(out=result[n][:, cols], in_=acc[n][b][:])
+                else:
+                    nc.vector.tensor_copy(out=result[n][:, cols], in_=acc[n][b][:])
+                nc.sync.dma_start(out=out_rows[n * P : (n + 1) * P, cols], in_=result[n][:, cols])
+
+        def run(stage, index, count, *more):
+            if 0 <= index < count:
+                stage(index, *more)
+
+        for step in range(W_TILES + X_TILES + 3):
+            run(exponential, step, W_TILES)
+            run(product_and_rowsum, step - 1, W_TILES)
+            run(quantise_w, step - 4, W_TILES)
+            run(reciprocal, step - 1, W_TILES)
+            run(regroup_w, step - 3, W_TILES)
+            run(normalise, step - 2, W_TILES)
+            run(transpose_w, step - 2, W_TILES)
+
+            n = step - (W_TILES + 3)
+            run(multiply, n, X_TILES)
+            run(gather_windows, n + 3, X_TILES)
+            run(transpose_x, n + 3, X_TILES)
+            run(regroup_x, n + 2, X_TILES)
+            run(quantise_x, n + 1, X_TILES)
+            run(empty_and_store, n, X_TILES)

@@ -52,8 +52,8 @@ def tile_connectlayer_kernel(tc, x, connect_w, connect_mask, out):
         keep = ctx.enter_context(tc.tile_pool(name="keep", bufs=1))
         work = ctx.enter_context(tc.tile_pool(name="work", bufs=3))
         results = ctx.enter_context(tc.tile_pool(name="results", bufs=4))
-        transposed = ctx.enter_context(tc.psum_pool(name="transposed", bufs=3))
-        sums = ctx.enter_context(tc.psum_pool(name="sums", bufs=5))
+        transposed = ctx.enter_context(tc.psum_pool(name="transposed", bufs=4))
+        sums = ctx.enter_context(tc.psum_pool(name="sums", bufs=4))
         ctx.enter_context(tc.manual_schedule())
 
         cw_in = []
@@ -106,13 +106,14 @@ def tile_connectlayer_kernel(tc, x, connect_w, connect_mask, out):
 
         def normalise(r):
             w_bf[r] = work.tile([P, K], BF16, name="w_bf")
-            nc.vector.tensor_scalar(
-                out=w_bf[r][:].rearrange("g (u q e) -> g u q e", u=2, e=2),
-                in0=prod[r][:].rearrange("g a c -> g (a c)").rearrange("g (q u e) -> g u q e", u=2, e=2),
-                scalar1=rinv[r][:, 0:1],
-                scalar2=None,
-                op0=ALU.mult,
-            )
+            sorted_w = w_bf[r][:].rearrange("g (u q e) -> g u q e", u=2, e=2)
+            product = prod[r][:].rearrange("g a c -> g (a c)").rearrange("g (q u e) -> g u q e", u=2, e=2)
+            if r % 3 == 0:
+                nc.scalar.activation(out=sorted_w, in_=product, func=ACT.Copy, scale=rinv[r][:, 0:1])
+            else:
+                nc.vector.tensor_scalar(
+                    out=sorted_w, in0=product, scalar1=rinv[r][:, 0:1], scalar2=None, op0=ALU.mult
+                )
 
         def transpose_w(r):
             wt[r] = transposed.tile([P, 2, P], F32, name="wt", tag="bank")
@@ -134,15 +135,15 @@ def tile_connectlayer_kernel(tc, x, connect_w, connect_mask, out):
                 in_=w_grouped[r][:],
             )
 
-        def gather_windows(n):
-            xc[n] = work.tile([P, COLS], BF16, name="xc")
-            for j in range(2):
-                nc.vector.tensor_copy(
-                    out=xc[n][:].bitcast(F32)[:, j * BANK : (j + 1) * BANK].rearrange(
-                        "b (u r s) -> b u r s", u=2, r=PIXEL_ROWS
-                    ),
-                    in_=x_in[n][:].bitcast(F32).rearrange("b (r j s u) -> b j u r s", r=PIXEL_ROWS, j=2, u=2)[:, j],
-                )
+        def gather_windows(n, j):
+            if j == 0:
+                xc[n] = work.tile([P, COLS], BF16, name="xc")
+            nc.vector.tensor_copy(
+                out=xc[n][:].bitcast(F32)[:, j * BANK : (j + 1) * BANK].rearrange(
+                    "b (u r s) -> b u r s", u=2, r=PIXEL_ROWS
+                ),
+                in_=x_in[n][:].bitcast(F32).rearrange("b (r j s u) -> b j u r s", r=PIXEL_ROWS, j=2, u=2)[:, j],
+            )
 
         def transpose_x(n):
             xc_words = xc[n][:].bitcast(F32)
@@ -198,18 +199,18 @@ def tile_connectlayer_kernel(tc, x, connect_w, connect_mask, out):
                 stage(index, *more)
 
         for step in range(W_TILES + X_TILES + 3):
+            n = step - (W_TILES + 3)
+            run(transpose_w, step - 3, W_TILES)
+            run(transpose_x, n + 2, X_TILES)
             run(exponential, step, W_TILES)
             run(product_and_rowsum, step - 1, W_TILES)
+            run(normalise, step - 2, W_TILES)
+            run(regroup_w, step - 3, W_TILES)
+            run(gather_windows, n + 3, X_TILES, 0)
             run(quantise_w, step - 4, W_TILES)
             run(reciprocal, step - 1, W_TILES)
-            run(regroup_w, step - 3, W_TILES)
-            run(normalise, step - 2, W_TILES)
-            run(transpose_w, step - 2, W_TILES)
-
-            n = step - (W_TILES + 3)
+            run(gather_windows, n + 3, X_TILES, 1)
             run(multiply, n, X_TILES)
-            run(gather_windows, n + 3, X_TILES)
-            run(transpose_x, n + 3, X_TILES)
             run(regroup_x, n + 2, X_TILES)
             run(quantise_x, n + 1, X_TILES)
             run(empty_and_store, n, X_TILES)

@@ -69,10 +69,14 @@ def tile_connectlayer_kernel(tc, x, connect_w, connect_mask, out):
             cw_in.append(cw_t)
             mask_in.append(mask_t)
         x_in = []
-        for n in range(X_TILES):
+        for n in range(4):
             x_t = loads.tile([P, COLS], BF16, name="x%d" % n)
             nc.sync.dma_start(out=x_t[:], in_=x[n * P : (n + 1) * P, :])
-            x_in.append(x_t)
+            x_in.append(x_t[:])
+        for n in range(4, X_TILES, 2):
+            x_pair = loads.tile([P, 2, COLS], BF16, name="x%d" % n)
+            nc.sync.dma_start(out=x_pair[:], in_=x[n * P : (n + 2) * P, :].rearrange("(a b) c -> b a c", a=2))
+            x_in.extend([x_pair[:, 0, :], x_pair[:, 1, :]])
 
         ident_f32 = const.tile([P, P], F32, name="ident_f32")
         make_identity(nc, ident_f32[:])
@@ -142,7 +146,7 @@ def tile_connectlayer_kernel(tc, x, connect_w, connect_mask, out):
                 out=xc[n][:].bitcast(F32)[:, j * BANK : (j + 1) * BANK].rearrange(
                     "b (u r s) -> b u r s", u=2, r=PIXEL_ROWS
                 ),
-                in_=x_in[n][:].bitcast(F32).rearrange("b (r j s u) -> b j u r s", r=PIXEL_ROWS, j=2, u=2)[:, j],
+                in_=x_in[n].bitcast(F32).rearrange("b (r j s u) -> b j u r s", r=PIXEL_ROWS, j=2, u=2)[:, j],
             )
 
         def transpose_x(n):
@@ -192,7 +196,10 @@ def tile_connectlayer_kernel(tc, x, connect_w, connect_mask, out):
                     nc.scalar.copy(out=result[n][:, cols], in_=acc[n][b][:])
                 else:
                     nc.vector.tensor_copy(out=result[n][:, cols], in_=acc[n][b][:])
-                nc.sync.dma_start(out=out_rows[n * P : (n + 1) * P, cols], in_=result[n][:, cols])
+                if n in (0, X_TILES - 1):
+                    nc.sync.dma_start(out=out_rows[n * P : (n + 1) * P, cols], in_=result[n][:, cols])
+            if not (n in (0, X_TILES - 1)):
+                nc.sync.dma_start(out=out_rows[n * P : (n + 1) * P, :], in_=result[n][:])
 
         def run(stage, index, count, *more):
             if 0 <= index < count:

@@ -80,6 +80,8 @@ def tile_connectlayer_kernel(tc, x, connect_w, connect_mask, out):
 
         ident_f32 = const.tile([P, P], F32, name="ident_f32")
         make_identity(nc, ident_f32[:])
+        ones = const.tile([P, BANK], BF16, name="ones")
+        nc.gpsimd.memset(ones[:], 1.0)
 
         w_codes = keep.tile([P, OUT_COLS], U32, name="w_codes", align_bytes=64)
         w_scales = keep.tile([P, OUT_COLS], U8, name="w_scales", align_bytes=64)
@@ -201,6 +203,10 @@ def tile_connectlayer_kernel(tc, x, connect_w, connect_mask, out):
             if not (n in (0, X_TILES - 1)):
                 nc.sync.dma_start(out=out_rows[n * P : (n + 1) * P, :], in_=result[n][:])
 
+        def warm_up():
+            idle = sums.tile([P, BANK], F32, name="idle", tag="acc")
+            nc.tensor.matmul(idle[:], lhsT=ones[:, 0:P], rhs=ones[:], start=True, stop=True)
+
         def run(stage, index, count, *more):
             if 0 <= index < count:
                 stage(index, *more)
@@ -209,6 +215,9 @@ def tile_connectlayer_kernel(tc, x, connect_w, connect_mask, out):
             n = step - (W_TILES + 3)
             run(transpose_w, step - 3, W_TILES)
             run(transpose_x, n + 2, X_TILES)
+            if -3 <= n < 0:
+                warm_up()
+                warm_up()
             run(exponential, step, W_TILES)
             run(product_and_rowsum, step - 1, W_TILES)
             run(normalise, step - 2, W_TILES)

@@ -192,16 +192,17 @@ def tile_connectlayer_kernel(tc, x, connect_w, connect_mask, out):
 
         def empty_and_store(n):
             result[n] = results.tile([P, OUT_COLS], F32, name="result")
+            stored = 0
             for b in range(BANKS_OUT):
                 cols = slice(b * BANK, (b + 1) * BANK)
                 if (n * BANKS_OUT + b) % 2 == 0:
                     nc.scalar.copy(out=result[n][:, cols], in_=acc[n][b][:])
                 else:
                     nc.vector.tensor_copy(out=result[n][:, cols], in_=acc[n][b][:])
-                if n in (0, X_TILES - 1):
-                    nc.sync.dma_start(out=out_rows[n * P : (n + 1) * P, cols], in_=result[n][:, cols])
-            if not (n in (0, X_TILES - 1)):
-                nc.sync.dma_start(out=out_rows[n * P : (n + 1) * P, :], in_=result[n][:])
+                if b == BANKS_OUT - 1 or n == 0 or (n == X_TILES - 1 and b == BANKS_OUT - 2):
+                    ready = slice(stored, (b + 1) * BANK)
+                    nc.sync.dma_start(out=out_rows[n * P : (n + 1) * P, ready], in_=result[n][:, ready])
+                    stored = (b + 1) * BANK
 
         def warm_up():
             idle = sums.tile([P, BANK], F32, name="idle", tag="acc")
@@ -215,8 +216,9 @@ def tile_connectlayer_kernel(tc, x, connect_w, connect_mask, out):
             n = step - (W_TILES + 3)
             run(transpose_w, step - 3, W_TILES)
             run(transpose_x, n + 2, X_TILES)
-            if -3 <= n < 0:
+            if -5 <= n < 0:
                 warm_up()
+            if -5 <= n < -1:
                 warm_up()
             run(exponential, step, W_TILES)
             run(product_and_rowsum, step - 1, W_TILES)

from contextlib import ExitStack

import concourse.mybir as mybir
from concourse.masks import make_identity

F32 = mybir.dt.float32
BF16 = mybir.dt.bfloat16
U32 = mybir.dt.uint32
U8 = mybir.dt.uint8
FP8X4 = mybir.dt.float8_e4m3fn_x4
ACT = mybir.ActivationFunctionType
ALU = mybir.AluOpType

P = 128
PACK = 4
K = P * PACK
BANK = 512

BATCH = 1024
COLS = 2048
PIXEL_ROWS = 16
ROW = COLS // PIXEL_ROWS
RUN = ROW // 2
WINDOW_ROWS = PIXEL_ROWS // 2
WINDOWS = 4
G = 384
OUT_COLS = WINDOWS * G
HALF = COLS // 2
SPAN = HALF - RUN

W_TILES = OUT_COLS // P
X_TILES = BATCH // P
BANKS_OUT = OUT_COLS // BANK

CUTS = sorted(set(range(0, OUT_COLS + 1, G)) | set(range(0, OUT_COLS + 1, BANK // 2)))

FLOPS = 2 * BATCH * OUT_COLS * K
BYTES = 2 * BATCH * COLS + 2 * 2 * OUT_COLS * K + 4 * BATCH * OUT_COLS


def window_view(half_rows):
    return half_rows[:].rearrange("g (a s) -> g a s", s=ROW)[:, :, 0:RUN]


def tile_connectlayer_kernel(tc, x, connect_w, connect_mask, out):
    nc = tc.nc
    out_rows = out.rearrange("b r s -> b (r s)")

    with ExitStack() as ctx:
        const = ctx.enter_context(tc.tile_pool(name="const", bufs=1))
        loads = ctx.enter_context(tc.tile_pool(name="loads", bufs=1))
        keep = ctx.enter_context(tc.tile_pool(name="keep", bufs=1))
        work = ctx.enter_context(tc.tile_pool(name="work", bufs=3))
        results = ctx.enter_context(tc.tile_pool(name="results", bufs=4))
        transposed = ctx.enter_context(tc.psum_pool(name="transposed", bufs=4))
        sums = ctx.enter_context(tc.psum_pool(name="sums", bufs=4))
        ctx.enter_context(tc.manual_schedule())

        cw_in = []
        mask_in = []
        for r in range(W_TILES):
            i, j = divmod(r * P // G, 2)
            rows = slice(r * P, (r + 1) * P)
            cols = slice(i * HALF + j * RUN, i * HALF + j * RUN + SPAN)
            cw_t = loads.tile([P, HALF], BF16, name="cw%d" % r)
            nc.sync.dma_start(out=cw_t[:, 0:SPAN], in_=connect_w[rows, cols])
            mask_t = loads.tile([P, HALF], BF16, name="mask%d" % r)
            nc.sync.dma_start(out=mask_t[:, 0:SPAN], in_=connect_mask[rows, cols])
            cw_in.append(cw_t)
            mask_in.append(mask_t)
        x_in = []
        for n in range(4):
            x_t = loads.tile([P, COLS], BF16, name="x%d" % n)
            nc.sync.dma_start(out=x_t[:], in_=x[n * P : (n + 1) * P, :])
            x_in.append(x_t[:])
        for n in range(4, X_TILES, 2):
            x_pair = loads.tile([P, 2, COLS], BF16, name="x%d" % n)
            nc.sync.dma_start(out=x_pair[:], in_=x[n * P : (n + 2) * P, :].rearrange("(a b) c -> b a c", a=2))
            x_in.extend([x_pair[:, 0, :], x_pair[:, 1, :]])

        ident_f32 = const.tile([P, P], F32, name="ident_f32")
        make_identity(nc, ident_f32[:])
        ones = const.tile([P, BANK], BF16, name="ones")
        nc.gpsimd.memset(ones[:], 1.0)

        w_codes = keep.tile([P, OUT_COLS], U32, name="w_codes", align_bytes=64)
        w_scales = keep.tile([P, OUT_COLS], U8, name="w_scales", align_bytes=64)

        expw, prod, rowsum, rinv, w_bf, wt, w_grouped = {}, {}, {}, {}, {}, {}, {}
        xc, xt, x_grouped, x_codes, x_scales, acc, result = {}, {}, {}, {}, {}, {}, {}

        def exponential(r):
            expw[r] = work.tile([P, WINDOW_ROWS, RUN], F32, name="expw")
            nc.scalar.activation(out=expw[r][:], in_=window_view(cw_in[r]), func=ACT.Exp)

        def product_and_rowsum(r):
            prod[r] = work.tile([P, WINDOW_ROWS, RUN], F32, name="prod")
            rowsum[r] = work.tile([P, 1], F32, name="rowsum")
            nc.vector.scalar_tensor_tensor(
                out=prod[r][:],
                in0=expw[r][:],
                scalar=1.0,
                in1=window_view(mask_in[r]),
                op0=ALU.mult,
                op1=ALU.mult,
                accum_out=rowsum[r][:],
            )

        def reciprocal(r):
            rinv[r] = work.tile([P, 1], F32, name="rinv")
            nc.vector.reciprocal(out=rinv[r][:], in_=rowsum[r][:])

        def normalise(r):
            w_bf[r] = work.tile([P, K], BF16, name="w_bf")
            sorted_w = w_bf[r][:].rearrange("g (u q e) -> g u q e", u=2, e=2)
            product = prod[r][:].rearrange("g a c -> g (a c)").rearrange("g (q u e) -> g u q e", u=2, e=2)
            if r % 3 == 0:
                nc.scalar.activation(out=sorted_w, in_=product, func=ACT.Copy, scale=rinv[r][:, 0:1])
            else:
                nc.vector.tensor_scalar(
                    out=sorted_w, in0=product, scalar1=rinv[r][:, 0:1], scalar2=None, op0=ALU.mult
                )

        def transpose_w(r):
            wt[r] = transposed.tile([P, 2, P], F32, name="wt", tag="bank")
            words = w_bf[r][:].bitcast(F32)
            for u in range(2):
                nc.tensor.transpose(wt[r][:, u, :], words[:, u * P : (u + 1) * P], ident_f32[:])

        def regroup_w(r):
            w_grouped[r] = work.tile([P, K], BF16, name="w_grouped", align_bytes=64)
            nc.scalar.copy(
                out=w_grouped[r][:].bitcast(F32).rearrange("q (g u) -> q g u", u=2),
                in_=wt[r][:].rearrange("q u g -> q g u"),
            )

        def quantise_w(r):
            nc.vector.quantize_mx(
                out=w_codes[:, r * P : (r + 1) * P].bitcast(FP8X4),
                scales=w_scales[:, r * P : (r + 1) * P],
                in_=w_grouped[r][:],
            )

        def gather_windows(n, j):
            if j == 0:
                xc[n] = work.tile([P, COLS], BF16, name="xc")
            nc.vector.tensor_copy(
                out=xc[n][:].bitcast(F32)[:, j * BANK : (j + 1) * BANK].rearrange(
                    "b (u r s) -> b u r s", u=2, r=PIXEL_ROWS
                ),
                in_=x_in[n].bitcast(F32).rearrange("b (r j s u) -> b j u r s", r=PIXEL_ROWS, j=2, u=2)[:, j],
            )

        def transpose_x(n):
            xc_words = xc[n][:].bitcast(F32)
            for j in range(2):
                xt[n, j] = transposed.tile([P, PACK, P], F32, name="xt", tag="bank")
                for i in range(2):
                    for u in range(2):
                        first = ((j * 2 + u) * 2 + i) * P
                        nc.tensor.transpose(xt[n, j][:, i * 2 + u, :], xc_words[:, first : first + P], ident_f32[:])

        def regroup_x(n):
            x_grouped[n] = work.tile([P, COLS], BF16, name="x_grouped", align_bytes=64)
            xg_words = x_grouped[n][:].bitcast(F32)
            for j in range(2):
                nc.scalar.copy(
                    out=xg_words[:, j * BANK : (j + 1) * BANK].rearrange("q (i b u) -> q i b u", i=2, u=2),
                    in_=xt[n, j][:].rearrange("q (i u) b -> q i b u", u=2),
                )

        def quantise_x(n):
            x_codes[n] = work.tile([P, BANK], U32, name="x_codes", align_bytes=64)
            x_scales[n] = work.tile([P, BANK], U8, name="x_scales", align_bytes=64)
            nc.vector.quantize_mx(out=x_codes[n][:].bitcast(FP8X4), scales=x_scales[n][:], in_=x_grouped[n][:])

        def multiply(n):
            acc[n] = [sums.tile([P, BANK], F32, name="acc%d" % b, tag="acc") for b in range(BANKS_OUT)]
            for c0, c1 in zip(CUTS[:-1], CUTS[1:]):
                i, j = divmod(c0 // G, 2)
                slot = slice((2 * j + i) * P, (2 * j + i + 1) * P)
                b = c0 // BANK
                nc.tensor.matmul_mx(
                    out=acc[n][b][:, c0 - b * BANK : c1 - b * BANK],
                    lhsT=x_codes[n][:, slot].bitcast(FP8X4),
                    lhsT_scale=x_scales[n][:, slot],
                    rhs=w_codes[:, c0:c1].bitcast(FP8X4),
                    rhs_scale=w_scales[:, c0:c1],
                    start=True,
                    stop=True,
                )

        def empty_and_store(n):
            result[n] = results.tile([P, OUT_COLS], F32, name="result")
            stored = 0
            for b in range(BANKS_OUT):
                cols = slice(b * BANK, (b + 1) * BANK)
                if (n * BANKS_OUT + b) % 2 == 0:
                    nc.scalar.copy(out=result[n][:, cols], in_=acc[n][b][:])
                else:
                    nc.vector.tensor_copy(out=result[n][:, cols], in_=acc[n][b][:])
                if b == BANKS_OUT - 1 or n == 0 or (n == X_TILES - 1 and b == BANKS_OUT - 2):
                    ready = slice(stored, (b + 1) * BANK)
                    nc.sync.dma_start(out=out_rows[n * P : (n + 1) * P, ready], in_=result[n][:, ready])
                    stored = (b + 1) * BANK

        def warm_up():
            idle = sums.tile([P, BANK], F32, name="idle", tag="acc")
            nc.tensor.matmul(idle[:], lhsT=ones[:, 0:P], rhs=ones[:], start=True, stop=True)

        def run(stage, index, count, *more):
            if 0 <= index < count:
                stage(index, *more)

        for step in range(W_TILES + X_TILES + 3):
            n = step - (W_TILES + 3)
            run(transpose_w, step - 3, W_TILES)
            run(transpose_x, n + 2, X_TILES)
            if -5 <= n < 0:
                warm_up()
            if -5 <= n < -1:
                warm_up()
            run(exponential, step, W_TILES)
            run(product_and_rowsum, step - 1, W_TILES)
            run(normalise, step - 2, W_TILES)
            run(regroup_w, step - 3, W_TILES)
            run(gather_windows, n + 3, X_TILES, 0)
            run(quantise_w, step - 4, W_TILES)
            run(reciprocal, step - 1, W_TILES)
            run(gather_windows, n + 3, X_TILES, 1)
            run(multiply, n, X_TILES)
            run(regroup_x, n + 2, X_TILES)
            run(quantise_x, n + 1, X_TILES)
            run(empty_and_store, n, X_TILES)
